import numpy as np
import ml_dtypes

BF16 = ml_dtypes.bfloat16


def bf(x):
    return np.asarray(x, np.float32).astype(BF16)


def f32(x):
    return np.asarray(x, np.float32)


def f64(x):
    return np.asarray(x).astype(np.float64)


def striped(idx):
    return np.tile(idx.reshape(-1, 16).T, (8, 1))


C, S, N, H, M = 512, 4096, 512, 2, 1024
EPS = 1e-8


def setup_inputs():
    w_e = f32(np.random.standard_normal((C, S)) + 0.5 * np.random.standard_normal((C, 1)))
    w_v = bf(np.random.standard_normal((C, M)) / np.sqrt(C))
    idx = np.random.permutation(np.tile(np.arange(S), 2))[:N]
    return {"w_e": w_e, "w_v": w_v, "offs": striped(idx)}


def reference(w_e, w_v, offs):
    idx = offs[:16].T.reshape(-1)
    t = f64(w_e)
    neg_e = -(t.sum(axis=1, keepdims=True) / (S + EPS))
    diff = t[:, idx] + neg_e
    return f64(w_v).T @ diff

@@ -1,0 +1,76 @@
+import concourse.mybir as mybir
+
+F32, BF16, U16 = mybir.dt.float32, mybir.dt.bfloat16, mybir.dt.uint16
+ADD, MULT = mybir.AluOpType.add, mybir.AluOpType.mult
+COPY = mybir.ActivationFunctionType.Copy
+X, XY = mybir.AxisListType.X, mybir.AxisListType.XY
+
+P = 128
+C, S, N, M = 512, 4096, 512, 1024
+EPS = 1e-8
+C_BLOCKS = C // P
+M_BLOCKS = M // P
+CHUNK = 1024
+CHUNKS = S // CHUNK
+HALF = CHUNK // 2
+LINE = 8
+
+FLOPS = 2 * C * M * N
+
+
+def tile_pgd_kernel(tc, w_e, w_v, offs, out):
+    nc = tc.nc
+    with (
+        tc.tile_pool(name="held", bufs=1) as held,
+        tc.tile_pool(name="work", bufs=2) as work,
+        tc.psum_pool(name="psum", bufs=1) as psum,
+    ):
+        offsets = held.tile([P, N // 16], U16, name="offsets")
+        nc.sync.dma_start(offsets[:], offs)
+
+        tables = [held.tile([P, S], F32, name=f"table{cb}") for cb in range(C_BLOCKS)]
+        values = [held.tile([P, M], BF16, name=f"values{cb}") for cb in range(C_BLOCKS)]
+        for cb in range(C_BLOCKS):
+            rows = slice(cb * P, (cb + 1) * P)
+            for k in range(CHUNKS):
+                cols = slice(k * CHUNK, (k + 1) * CHUNK)
+                nc.sync.dma_start(tables[cb][:, cols], w_e[rows, cols])
+            nc.sync.dma_start(values[cb][:], w_v[rows, :])
+
+        banks = [psum.tile([P, N], F32, name=f"bank{mb}") for mb in range(M_BLOCKS)]
+
+        for cb in range(C_BLOCKS):
+            parts = work.tile([P, 2, LINE], F32, name="parts")
+            for k in range(CHUNKS):
+                lo = k * CHUNK
+                nc.vector.tensor_reduce(
+                    out=parts[:, 0, k : k + 1], in_=tables[cb][:, lo : lo + HALF], axis=X, op=ADD
+                )
+                unused = work.tile([P, HALF], F32, name="unused")
+                nc.scalar.activation(
+                    out=unused[:], in_=tables[cb][:, lo + HALF : lo + CHUNK], func=COPY,
+                    accum_out=parts[:, 1, k : k + 1],
+                )
+            neg_sum = work.tile([P, 1], F32, name="neg_sum")
+            nc.vector.tensor_reduce(out=neg_sum[:], in_=parts[:, :, 0:CHUNKS], axis=XY, op=ADD, negate=True)
+            neg_e = work.tile([P, N], F32, name="neg_e")
+            nc.vector.tensor_scalar_mul(neg_e[:], neg_sum[:, 0:1].to_broadcast([P, N]), 1.0 / (S + EPS))
+
+            diff = work.tile([P, N], F32, name="diff")
+            nc.vector.tensor_tensor(diff[:], tables[cb][:].indirect(offsets[:]), neg_e[:], ADD)
+            diff_bf = work.tile([P, N], BF16, name="diff_bf")
+            nc.vector.tensor_copy(diff_bf[:], diff[:])
+
+            for mb in range(M_BLOCKS):
+                nc.tensor.matmul(
+                    banks[mb][:], values[cb][:, mb * P : (mb + 1) * P], diff_bf[:],
+                    start=(cb == 0), stop=(cb == C_BLOCKS - 1),
+                )
+
+        for mb in range(M_BLOCKS):
+            staged = held.tile([P, N], F32, name=f"staged{mb}")
+            if mb % 2 == 0:
+                nc.vector.tensor_copy(staged[:], banks[mb][:])
+            else:
+                nc.scalar.activation(staged[:], banks[mb][:], COPY)
+            nc.sync.dma_start(out[mb * P : (mb + 1) * P, :], staged[:])

@@ -1,7 +1,7 @@
 import concourse.mybir as mybir
 
 F32, BF16, U16 = mybir.dt.float32, mybir.dt.bfloat16, mybir.dt.uint16
-ADD, MULT = mybir.AluOpType.add, mybir.AluOpType.mult
+ADD = mybir.AluOpType.add
 COPY = mybir.ActivationFunctionType.Copy
 X, XY = mybir.AxisListType.X, mybir.AxisListType.XY
 
@@ -10,12 +10,15 @@ C, S, N, M = 512, 4096, 512, 1024
 EPS = 1e-8
 C_BLOCKS = C // P
 M_BLOCKS = M // P
-CHUNK = 1024
-CHUNKS = S // CHUNK
-HALF = CHUNK // 2
 LINE = 8
-
+SHORT = 256
 FLOPS = 2 * C * M * N
+
+
+def load_widths(cb):
+    if cb < C_BLOCKS - 1:
+        return [S // 2, S // 2]
+    return [S // 2, S // 4, S // 8, SHORT, SHORT]
 
 
 def tile_pgd_kernel(tc, w_e, w_v, offs, out):
@@ -32,27 +35,31 @@ def tile_pgd_kernel(tc, w_e, w_v, offs, out):
         values = [held.tile([P, M], BF16, name=f"values{cb}") for cb in range(C_BLOCKS)]
         for cb in range(C_BLOCKS):
             rows = slice(cb * P, (cb + 1) * P)
-            for k in range(CHUNKS):
-                cols = slice(k * CHUNK, (k + 1) * CHUNK)
-                nc.sync.dma_start(tables[cb][:, cols], w_e[rows, cols])
+            lo = 0
+            for width in load_widths(cb):
+                nc.sync.dma_start(tables[cb][:, lo : lo + width], w_e[rows, lo : lo + width])
+                lo += width
             nc.sync.dma_start(values[cb][:], w_v[rows, :])
 
         banks = [psum.tile([P, N], F32, name=f"bank{mb}") for mb in range(M_BLOCKS)]
 
         for cb in range(C_BLOCKS):
-            parts = work.tile([P, 2, LINE], F32, name="parts")
-            for k in range(CHUNKS):
-                lo = k * CHUNK
-                nc.vector.tensor_reduce(
-                    out=parts[:, 0, k : k + 1], in_=tables[cb][:, lo : lo + HALF], axis=X, op=ADD
-                )
-                unused = work.tile([P, HALF], F32, name="unused")
-                nc.scalar.activation(
-                    out=unused[:], in_=tables[cb][:, lo + HALF : lo + CHUNK], func=COPY,
-                    accum_out=parts[:, 1, k : k + 1],
-                )
+            parts = work.tile([P, 2 * LINE], F32, name="parts")
+            nc.vector.memset(parts[:], 0.0)
+            lo = 0
+            for k, width in enumerate(load_widths(cb)):
+                hi = lo + width
+                mid = hi if width <= SHORT else lo + 3 * width // 8
+                nc.vector.tensor_reduce(out=parts[:, k : k + 1], in_=tables[cb][:, lo:mid], axis=X, op=ADD)
+                if mid < hi:
+                    unused = work.tile([P, 5 * S // 16], F32, name="unused")
+                    nc.scalar.activation(
+                        out=unused[:, 0 : hi - mid], in_=tables[cb][:, mid:hi], func=COPY,
+                        accum_out=parts[:, LINE + k : LINE + k + 1],
+                    )
+                lo = hi
             neg_sum = work.tile([P, 1], F32, name="neg_sum")
-            nc.vector.tensor_reduce(out=neg_sum[:], in_=parts[:, :, 0:CHUNKS], axis=XY, op=ADD, negate=True)
+            nc.vector.tensor_reduce(out=neg_sum[:], in_=parts[:], axis=X, op=ADD, negate=True)
             neg_e = work.tile([P, N], F32, name="neg_e")
             nc.vector.tensor_scalar_mul(neg_e[:], neg_sum[:, 0:1].to_broadcast([P, N]), 1.0 / (S + EPS))
 
@@ -71,6 +78,7 @@ def tile_pgd_kernel(tc, w_e, w_v, offs, out):
             staged = held.tile([P, N], F32, name=f"staged{mb}")
             if mb % 2 == 0:
                 nc.vector.tensor_copy(staged[:], banks[mb][:])
+                nc.sync.dma_start(out[mb * P : (mb + 1) * P, :], staged[:])
             else:
                 nc.scalar.activation(staged[:], banks[mb][:], COPY)
-            nc.sync.dma_start(out[mb * P : (mb + 1) * P, :], staged[:])
+                nc.scalar.dma_start(out[mb * P : (mb + 1) * P, :], staged[:])

@@ -1,7 +1,7 @@
 import concourse.mybir as mybir
 
 F32, BF16, U16 = mybir.dt.float32, mybir.dt.bfloat16, mybir.dt.uint16
-ADD = mybir.AluOpType.add
+ADD, MULT = mybir.AluOpType.add, mybir.AluOpType.mult
 COPY = mybir.ActivationFunctionType.Copy
 X, XY = mybir.AxisListType.X, mybir.AxisListType.XY
 
@@ -10,15 +10,13 @@ C, S, N, M = 512, 4096, 512, 1024
 EPS = 1e-8
 C_BLOCKS = C // P
 M_BLOCKS = M // P
+M_PAIRS = M_BLOCKS // 2
+CHUNK = 1024
+CHUNKS = S // CHUNK
+HALF = CHUNK // 2
 LINE = 8
-SHORT = 256
+
 FLOPS = 2 * C * M * N
-
-
-def load_widths(cb):
-    if cb < C_BLOCKS - 1:
-        return [S // 2, S // 2]
-    return [S // 2, S // 4, S // 8, SHORT, SHORT]
 
 
 def tile_pgd_kernel(tc, w_e, w_v, offs, out):
@@ -35,31 +33,27 @@ def tile_pgd_kernel(tc, w_e, w_v, offs, out):
         values = [held.tile([P, M], BF16, name=f"values{cb}") for cb in range(C_BLOCKS)]
         for cb in range(C_BLOCKS):
             rows = slice(cb * P, (cb + 1) * P)
-            lo = 0
-            for width in load_widths(cb):
-                nc.sync.dma_start(tables[cb][:, lo : lo + width], w_e[rows, lo : lo + width])
-                lo += width
+            for k in range(CHUNKS):
+                cols = slice(k * CHUNK, (k + 1) * CHUNK)
+                nc.sync.dma_start(tables[cb][:, cols], w_e[rows, cols])
             nc.sync.dma_start(values[cb][:], w_v[rows, :])
 
         banks = [psum.tile([P, N], F32, name=f"bank{mb}") for mb in range(M_BLOCKS)]
 
         for cb in range(C_BLOCKS):
-            parts = work.tile([P, 2 * LINE], F32, name="parts")
-            nc.vector.memset(parts[:], 0.0)
-            lo = 0
-            for k, width in enumerate(load_widths(cb)):
-                hi = lo + width
-                mid = hi if width <= SHORT else lo + 3 * width // 8
-                nc.vector.tensor_reduce(out=parts[:, k : k + 1], in_=tables[cb][:, lo:mid], axis=X, op=ADD)
-                if mid < hi:
-                    unused = work.tile([P, 5 * S // 16], F32, name="unused")
-                    nc.scalar.activation(
-                        out=unused[:, 0 : hi - mid], in_=tables[cb][:, mid:hi], func=COPY,
-                        accum_out=parts[:, LINE + k : LINE + k + 1],
-                    )
-                lo = hi
+            parts = work.tile([P, 2, LINE], F32, name="parts")
+            for k in range(CHUNKS):
+                lo = k * CHUNK
+                nc.vector.tensor_reduce(
+                    out=parts[:, 0, k : k + 1], in_=tables[cb][:, lo : lo + HALF], axis=X, op=ADD
+                )
+                unused = work.tile([P, HALF], F32, name="unused")
+                nc.scalar.activation(
+                    out=unused[:], in_=tables[cb][:, lo + HALF : lo + CHUNK], func=COPY,
+                    accum_out=parts[:, 1, k : k + 1],
+                )
             neg_sum = work.tile([P, 1], F32, name="neg_sum")
-            nc.vector.tensor_reduce(out=neg_sum[:], in_=parts[:], axis=X, op=ADD, negate=True)
+            nc.vector.tensor_reduce(out=neg_sum[:], in_=parts[:, :, 0:CHUNKS], axis=XY, op=ADD, negate=True)
             neg_e = work.tile([P, N], F32, name="neg_e")
             nc.vector.tensor_scalar_mul(neg_e[:], neg_sum[:, 0:1].to_broadcast([P, N]), 1.0 / (S + EPS))
 
@@ -69,16 +63,14 @@ def tile_pgd_kernel(tc, w_e, w_v, offs, out):
             nc.vector.tensor_copy(diff_bf[:], diff[:])
 
             for mb in range(M_BLOCKS):
+                i, r = divmod(mb, 2)
                 nc.tensor.matmul(
-                    banks[mb][:], values[cb][:, mb * P : (mb + 1) * P], diff_bf[:],
+                    banks[mb][:], values[cb][:, 2 * P * i + r : 2 * P * (i + 1) : 2], diff_bf[:],
                     start=(cb == 0), stop=(cb == C_BLOCKS - 1),
                 )
 
-        for mb in range(M_BLOCKS):
-            staged = held.tile([P, N], F32, name=f"staged{mb}")
-            if mb % 2 == 0:
-                nc.vector.tensor_copy(staged[:], banks[mb][:])
-                nc.sync.dma_start(out[mb * P : (mb + 1) * P, :], staged[:])
-            else:
-                nc.scalar.activation(staged[:], banks[mb][:], COPY)
-                nc.scalar.dma_start(out[mb * P : (mb + 1) * P, :], staged[:])
+        for i in range(M_PAIRS):
+            staged = held.tile([P, 2 * N], F32, name=f"staged{i}")
+            nc.vector.tensor_copy(staged[:, 0:N], banks[2 * i][:])
+            nc.scalar.activation(staged[:, N : 2 * N], banks[2 * i + 1][:], COPY)
+            nc.sync.dma_start(out[2 * P * i : 2 * P * (i + 1), :].rearrange("(p r) j -> p (r j)", r=2), staged[:])

@@ -10,11 +10,12 @@ C, S, N, M = 512, 4096, 512, 1024
 EPS = 1e-8
 C_BLOCKS = C // P
 M_BLOCKS = M // P
-M_PAIRS = M_BLOCKS // 2
 CHUNK = 1024
 CHUNKS = S // CHUNK
 HALF = CHUNK // 2
 LINE = 8
+PIECE = 256
+PIECES = N // PIECE
 
 FLOPS = 2 * C * M * N
 
@@ -54,23 +55,28 @@ def tile_pgd_kernel(tc, w_e, w_v, offs, out):
                 )
             neg_sum = work.tile([P, 1], F32, name="neg_sum")
             nc.vector.tensor_reduce(out=neg_sum[:], in_=parts[:, :, 0:CHUNKS], axis=XY, op=ADD, negate=True)
-            neg_e = work.tile([P, N], F32, name="neg_e")
-            nc.vector.tensor_scalar_mul(neg_e[:], neg_sum[:, 0:1].to_broadcast([P, N]), 1.0 / (S + EPS))
+            neg_e = work.tile([P, PIECE], F32, name="neg_e")
+            nc.vector.tensor_scalar_mul(neg_e[:], neg_sum[:, 0:1].to_broadcast([P, PIECE]), 1.0 / (S + EPS))
 
-            diff = work.tile([P, N], F32, name="diff")
-            nc.vector.tensor_tensor(diff[:], tables[cb][:].indirect(offsets[:]), neg_e[:], ADD)
-            diff_bf = work.tile([P, N], BF16, name="diff_bf")
-            nc.vector.tensor_copy(diff_bf[:], diff[:])
+            for q in range(PIECES):
+                diff = work.tile([P, PIECE], F32, name="diff")
+                piece_offsets = offsets[:, q * PIECE // 16 : (q + 1) * PIECE // 16]
+                nc.vector.tensor_tensor(diff[:], tables[cb][:].indirect(piece_offsets), neg_e[:], ADD)
+                diff_bf = work.tile([P, PIECE], BF16, name="diff_bf")
+                if q < PIECES - 1:
+                    nc.scalar.activation(diff_bf[:], diff[:], COPY)
+                else:
+                    nc.vector.tensor_copy(diff_bf[:], diff[:])
+                for mb in range(M_BLOCKS):
+                    nc.tensor.matmul(
+                        banks[mb][:, q * PIECE : (q + 1) * PIECE], values[cb][:, mb * P : (mb + 1) * P], diff_bf[:],
+                        start=(cb == 0 and q == 0), stop=(cb == C_BLOCKS - 1 and q == PIECES - 1),
+                    )
 
-            for mb in range(M_BLOCKS):
-                i, r = divmod(mb, 2)
-                nc.tensor.matmul(
-                    banks[mb][:], values[cb][:, 2 * P * i + r : 2 * P * (i + 1) : 2], diff_bf[:],
-                    start=(cb == 0), stop=(cb == C_BLOCKS - 1),
-                )
-
-        for i in range(M_PAIRS):
-            staged = held.tile([P, 2 * N], F32, name=f"staged{i}")
-            nc.vector.tensor_copy(staged[:, 0:N], banks[2 * i][:])
-            nc.scalar.activation(staged[:, N : 2 * N], banks[2 * i + 1][:], COPY)
-            nc.sync.dma_start(out[2 * P * i : 2 * P * (i + 1), :].rearrange("(p r) j -> p (r j)", r=2), staged[:])
+        for mb in range(M_BLOCKS):
+            staged = held.tile([P, N], F32, name=f"staged{mb}")
+            if mb % 2 == 0:
+                nc.vector.tensor_copy(staged[:], banks[mb][:])
+            else:
+                nc.scalar.activation(staged[:], banks[mb][:], COPY)
+            nc.sync.dma_start(out[mb * P : (mb + 1) * P, :], staged[:])

@@ -3,21 +3,22 @@ import concourse.mybir as mybir
 F32, BF16, U16 = mybir.dt.float32, mybir.dt.bfloat16, mybir.dt.uint16
 ADD, MULT = mybir.AluOpType.add, mybir.AluOpType.mult
 COPY = mybir.ActivationFunctionType.Copy
-X, XY = mybir.AxisListType.X, mybir.AxisListType.XY
+X = mybir.AxisListType.X
 
 P = 128
 C, S, N, M = 512, 4096, 512, 1024
 EPS = 1e-8
 C_BLOCKS = C // P
 M_BLOCKS = M // P
-CHUNK = 1024
-CHUNKS = S // CHUNK
-HALF = CHUNK // 2
 LINE = 8
-PIECE = 256
-PIECES = N // PIECE
 
 FLOPS = 2 * C * M * N
+
+
+def load_widths(cb):
+    if cb < C_BLOCKS - 1:
+        return [S // 2, S // 2]
+    return [S // 4, S // 4, S // 4, S // 8, S // 8]
 
 
 def tile_pgd_kernel(tc, w_e, w_v, offs, out):
@@ -34,44 +35,49 @@ def tile_pgd_kernel(tc, w_e, w_v, offs, out):
         values = [held.tile([P, M], BF16, name=f"values{cb}") for cb in range(C_BLOCKS)]
         for cb in range(C_BLOCKS):
             rows = slice(cb * P, (cb + 1) * P)
-            for k in range(CHUNKS):
-                cols = slice(k * CHUNK, (k + 1) * CHUNK)
-                nc.sync.dma_start(tables[cb][:, cols], w_e[rows, cols])
+            lo = 0
+            for width in load_widths(cb):
+                nc.sync.dma_start(tables[cb][:, lo : lo + width], w_e[rows, lo : lo + width])
+                lo += width
             nc.sync.dma_start(values[cb][:], w_v[rows, :])
 
         banks = [psum.tile([P, N], F32, name=f"bank{mb}") for mb in range(M_BLOCKS)]
 
         for cb in range(C_BLOCKS):
-            parts = work.tile([P, 2, LINE], F32, name="parts")
-            for k in range(CHUNKS):
-                lo = k * CHUNK
-                nc.vector.tensor_reduce(
-                    out=parts[:, 0, k : k + 1], in_=tables[cb][:, lo : lo + HALF], axis=X, op=ADD
-                )
-                unused = work.tile([P, HALF], F32, name="unused")
-                nc.scalar.activation(
-                    out=unused[:], in_=tables[cb][:, lo + HALF : lo + CHUNK], func=COPY,
-                    accum_out=parts[:, 1, k : k + 1],
-                )
-            neg_sum = work.tile([P, 1], F32, name="neg_sum")
-            nc.vector.tensor_reduce(out=neg_sum[:], in_=parts[:, :, 0:CHUNKS], axis=XY, op=ADD, negate=True)
-            neg_e = work.tile([P, PIECE], F32, name="neg_e")
-            nc.vector.tensor_scalar_mul(neg_e[:], neg_sum[:, 0:1].to_broadcast([P, PIECE]), 1.0 / (S + EPS))
-
-            for q in range(PIECES):
-                diff = work.tile([P, PIECE], F32, name="diff")
-                piece_offsets = offsets[:, q * PIECE // 16 : (q + 1) * PIECE // 16]
-                nc.vector.tensor_tensor(diff[:], tables[cb][:].indirect(piece_offsets), neg_e[:], ADD)
-                diff_bf = work.tile([P, PIECE], BF16, name="diff_bf")
-                if q < PIECES - 1:
-                    nc.scalar.activation(diff_bf[:], diff[:], COPY)
-                else:
-                    nc.vector.tensor_copy(diff_bf[:], diff[:])
-                for mb in range(M_BLOCKS):
-                    nc.tensor.matmul(
-                        banks[mb][:, q * PIECE : (q + 1) * PIECE], values[cb][:, mb * P : (mb + 1) * P], diff_bf[:],
-                        start=(cb == 0 and q == 0), stop=(cb == C_BLOCKS - 1 and q == PIECES - 1),
+            parts = work.tile([P, 2 * LINE], F32, name="parts")
+            nc.vector.memset(parts[:], 0.0)
+            lo = 0
+            for k, width in enumerate(load_widths(cb)):
+                if lo < S // 2:
+                    copied = work.tile([P, S // 2], F32, name="copied")
+                    nc.scalar.activation(
+                        out=copied[:, 0:width], in_=tables[cb][:, lo : lo + width], func=COPY,
+                        accum_out=parts[:, k : k + 1],
                     )
+                else:
+                    mid = lo + width // 2
+                    folded = work.tile([P, S // 4], F32, name="folded")
+                    nc.vector.scalar_tensor_tensor(
+                        out=folded[:, 0 : width // 2], in0=tables[cb][:, lo:mid], scalar=1.0,
+                        in1=tables[cb][:, mid : lo + width], op0=MULT, op1=ADD,
+                        accum_out=parts[:, LINE + k : LINE + k + 1],
+                    )
+                lo += width
+            neg_sum = work.tile([P, 1], F32, name="neg_sum")
+            nc.vector.tensor_reduce(out=neg_sum[:], in_=parts[:], axis=X, op=ADD, negate=True)
+            neg_e = work.tile([P, N], F32, name="neg_e")
+            nc.vector.tensor_scalar_mul(neg_e[:], neg_sum[:, 0:1].to_broadcast([P, N]), 1.0 / (S + EPS))
+
+            diff = work.tile([P, N], F32, name="diff")
+            nc.vector.tensor_tensor(diff[:], tables[cb][:].indirect(offsets[:]), neg_e[:], ADD)
+            diff_bf = work.tile([P, N], BF16, name="diff_bf")
+            nc.vector.tensor_copy(diff_bf[:], diff[:])
+
+            for mb in range(M_BLOCKS):
+                nc.tensor.matmul(
+                    banks[mb][:], values[cb][:, mb * P : (mb + 1) * P], diff_bf[:],
+                    start=(cb == 0), stop=(cb == C_BLOCKS - 1),
+                )
 
         for mb in range(M_BLOCKS):
             staged = held.tile([P, N], F32, name=f"staged{mb}")

@@ -11,6 +11,7 @@ EPS = 1e-8
 C_BLOCKS = C // P
 M_BLOCKS = M // P
 LINE = 8
+PIECE = 256
 
 FLOPS = 2 * C * M * N
 
@@ -46,8 +47,13 @@ def tile_pgd_kernel(tc, w_e, w_v, offs, out):
         for cb in range(C_BLOCKS):
             parts = work.tile([P, 2 * LINE], F32, name="parts")
             nc.vector.memset(parts[:], 0.0)
+            earlier = work.tile([P, 1], F32, name="earlier")
+            newest = work.tile([P, 1], F32, name="newest")
             lo = 0
+            last_k = len(load_widths(cb)) - 1
             for k, width in enumerate(load_widths(cb)):
+                if k == last_k:
+                    nc.vector.tensor_reduce(out=earlier[:], in_=parts[:], axis=X, op=ADD)
                 if lo < S // 2:
                     copied = work.tile([P, S // 2], F32, name="copied")
                     nc.scalar.activation(
@@ -60,16 +66,21 @@ def tile_pgd_kernel(tc, w_e, w_v, offs, out):
                     nc.vector.scalar_tensor_tensor(
                         out=folded[:, 0 : width // 2], in0=tables[cb][:, lo:mid], scalar=1.0,
                         in1=tables[cb][:, mid : lo + width], op0=MULT, op1=ADD,
-                        accum_out=parts[:, LINE + k : LINE + k + 1],
+                        accum_out=newest[:] if k == last_k else parts[:, LINE + k : LINE + k + 1],
                     )
                 lo += width
-            neg_sum = work.tile([P, 1], F32, name="neg_sum")
-            nc.vector.tensor_reduce(out=neg_sum[:], in_=parts[:], axis=X, op=ADD, negate=True)
-            neg_e = work.tile([P, N], F32, name="neg_e")
-            nc.vector.tensor_scalar_mul(neg_e[:], neg_sum[:, 0:1].to_broadcast([P, N]), 1.0 / (S + EPS))
+            neg_e = work.tile([P, PIECE], F32, name="neg_e")
+            nc.vector.tensor_scalar(
+                out=neg_e[:], in0=earlier[:, 0:1].to_broadcast([P, PIECE]), scalar1=newest[:, 0:1],
+                scalar2=-1.0 / (S + EPS), op0=ADD, op1=MULT,
+            )
 
             diff = work.tile([P, N], F32, name="diff")
-            nc.vector.tensor_tensor(diff[:], tables[cb][:].indirect(offsets[:]), neg_e[:], ADD)
+            for lo in range(0, N, PIECE):
+                nc.vector.tensor_tensor(
+                    diff[:, lo : lo + PIECE],
+                    tables[cb][:].indirect(offsets[:, lo // 16 : (lo + PIECE) // 16]), neg_e[:], ADD,
+                )
             diff_bf = work.tile([P, N], BF16, name="diff_bf")
             nc.vector.tensor_copy(diff_bf[:], diff[:])
 

@@ -22,6 +22,14 @@ def load_widths(cb):
     return [S // 4, S // 4, S // 4, S // 8, S // 8]
 
 
+def store_groups():
+    groups = [(0, 1)]
+    while groups[-1][1] < M_BLOCKS:
+        end = groups[-1][1]
+        groups.append((end, 2 * end))
+    return groups
+
+
 def tile_pgd_kernel(tc, w_e, w_v, offs, out):
     nc = tc.nc
     with (
@@ -84,16 +92,19 @@ def tile_pgd_kernel(tc, w_e, w_v, offs, out):
             diff_bf = work.tile([P, N], BF16, name="diff_bf")
             nc.vector.tensor_copy(diff_bf[:], diff[:])
 
+            weights = values[cb][:].rearrange("c (p mb) -> c mb p", mb=M_BLOCKS)
             for mb in range(M_BLOCKS):
                 nc.tensor.matmul(
-                    banks[mb][:], values[cb][:, mb * P : (mb + 1) * P], diff_bf[:],
+                    banks[mb][:], weights[:, mb, :], diff_bf[:],
                     start=(cb == 0), stop=(cb == C_BLOCKS - 1),
                 )
 
-        for mb in range(M_BLOCKS):
-            staged = held.tile([P, N], F32, name=f"staged{mb}")
-            if mb % 2 == 0:
-                nc.vector.tensor_copy(staged[:], banks[mb][:])
-            else:
-                nc.scalar.activation(staged[:], banks[mb][:], COPY)
-            nc.sync.dma_start(out[mb * P : (mb + 1) * P, :], staged[:])
+        staged = held.tile([P, M_BLOCKS * N], F32, name="staged")
+        out_by_partition = out.rearrange("(p mb) j -> p (mb j)", mb=M_BLOCKS)
+        for first, end in store_groups():
+            for mb in range(first, end):
+                if mb % 2 == 0:
+                    nc.vector.tensor_copy(staged[:, mb * N : (mb + 1) * N], banks[mb][:])
+                else:
+                    nc.scalar.activation(staged[:, mb * N : (mb + 1) * N], banks[mb][:], COPY)
+            nc.sync.dma_start(out_by_partition[:, first * N : end * N], staged[:, first * N : end * N])

@@ -22,12 +22,12 @@ def load_widths(cb):
     return [S // 4, S // 4, S // 4, S // 8, S // 8]
 
 
-def store_groups():
-    groups = [(0, 1)]
-    while groups[-1][1] < M_BLOCKS:
-        end = groups[-1][1]
-        groups.append((end, 2 * end))
-    return groups
+def store_ranges():
+    ranges = [(0, N // 2)]
+    while ranges[-1][1] < M_BLOCKS * N:
+        hi = ranges[-1][1]
+        ranges.append((hi, 2 * hi))
+    return ranges
 
 
 def tile_pgd_kernel(tc, w_e, w_v, offs, out):
@@ -101,10 +101,12 @@ def tile_pgd_kernel(tc, w_e, w_v, offs, out):
 
         staged = held.tile([P, M_BLOCKS * N], F32, name="staged")
         out_by_partition = out.rearrange("(p mb) j -> p (mb j)", mb=M_BLOCKS)
-        for first, end in store_groups():
-            for mb in range(first, end):
+        for lo, hi in store_ranges():
+            for a in range(lo, hi, N):
+                b = min(a + N, hi)
+                mb = a // N
                 if mb % 2 == 0:
-                    nc.vector.tensor_copy(staged[:, mb * N : (mb + 1) * N], banks[mb][:])
+                    nc.vector.tensor_copy(staged[:, a:b], banks[mb][:, a - mb * N : b - mb * N])
                 else:
-                    nc.scalar.activation(staged[:, mb * N : (mb + 1) * N], banks[mb][:], COPY)
-            nc.sync.dma_start(out_by_partition[:, first * N : end * N], staged[:, first * N : end * N])
+                    nc.scalar.activation(staged[:, a:b], banks[mb][:, a - mb * N : b - mb * N], COPY)
+            nc.sync.dma_start(out_by_partition[:, lo:hi], staged[:, lo:hi])

@@ -42,13 +42,23 @@ def tile_pgd_kernel(tc, w_e, w_v, offs, out):
 
         tables = [held.tile([P, S], F32, name=f"table{cb}") for cb in range(C_BLOCKS)]
         values = [held.tile([P, M], BF16, name=f"values{cb}") for cb in range(C_BLOCKS)]
-        for cb in range(C_BLOCKS):
-            rows = slice(cb * P, (cb + 1) * P)
+
+        def load_table(cb):
             lo = 0
             for width in load_widths(cb):
-                nc.sync.dma_start(tables[cb][:, lo : lo + width], w_e[rows, lo : lo + width])
+                nc.sync.dma_start(tables[cb][:, lo : lo + width], w_e[cb * P : (cb + 1) * P, lo : lo + width])
                 lo += width
-            nc.sync.dma_start(values[cb][:], w_v[rows, :])
+
+        def load_values(cb):
+            nc.sync.dma_start(values[cb][:], w_v[cb * P : (cb + 1) * P, :])
+
+        for cb in range(C_BLOCKS - 1):
+            load_table(cb)
+        for cb in range(C_BLOCKS // 2):
+            load_values(cb)
+        load_table(C_BLOCKS - 1)
+        for cb in range(C_BLOCKS // 2, C_BLOCKS):
+            load_values(cb)
 
         banks = [psum.tile([P, N], F32, name=f"bank{mb}") for mb in range(M_BLOCKS)]
 
@@ -89,7 +99,7 @@ def tile_pgd_kernel(tc, w_e, w_v, offs, out):
                     diff[:, lo : lo + PIECE],
                     tables[cb][:].indirect(offsets[:, lo // 16 : (lo + PIECE) // 16]), neg_e[:], ADD,
                 )
-            diff_bf = work.tile([P, N], BF16, name="diff_bf")
+            diff_bf = held.tile([P, N], BF16, name=f"diff_bf{cb}")
             nc.vector.tensor_copy(diff_bf[:], diff[:])
 
             weights = values[cb][:].rearrange("c (p mb) -> c mb p", mb=M_BLOCKS)

@@ -63,15 +63,14 @@ def tile_pgd_kernel(tc, w_e, w_v, offs, out):
         banks = [psum.tile([P, N], F32, name=f"bank{mb}") for mb in range(M_BLOCKS)]
 
         for cb in range(C_BLOCKS):
-            parts = work.tile([P, 2 * LINE], F32, name="parts")
-            nc.vector.memset(parts[:], 0.0)
+            parts = work.tile([P, LINE], F32, name="parts")
             earlier = work.tile([P, 1], F32, name="earlier")
             newest = work.tile([P, 1], F32, name="newest")
             lo = 0
             last_k = len(load_widths(cb)) - 1
             for k, width in enumerate(load_widths(cb)):
                 if k == last_k:
-                    nc.vector.tensor_reduce(out=earlier[:], in_=parts[:], axis=X, op=ADD)
+                    nc.vector.tensor_reduce(out=earlier[:], in_=parts[:, 0:last_k], axis=X, op=ADD)
                 if lo < S // 2:
                     copied = work.tile([P, S // 2], F32, name="copied")
                     nc.scalar.activation(
@@ -84,7 +83,7 @@ def tile_pgd_kernel(tc, w_e, w_v, offs, out):
                     nc.vector.scalar_tensor_tensor(
                         out=folded[:, 0 : width // 2], in0=tables[cb][:, lo:mid], scalar=1.0,
                         in1=tables[cb][:, mid : lo + width], op0=MULT, op1=ADD,
-                        accum_out=newest[:] if k == last_k else parts[:, LINE + k : LINE + k + 1],
+                        accum_out=newest[:] if k == last_k else parts[:, k : k + 1],
                     )
                 lo += width
             neg_e = work.tile([P, PIECE], F32, name="neg_e")
@@ -94,13 +93,16 @@ def tile_pgd_kernel(tc, w_e, w_v, offs, out):
             )
 
             diff = work.tile([P, N], F32, name="diff")
+            by_scalar = N - PIECE if cb == C_BLOCKS - 1 else 0
+            diff_bf = held.tile([P, N], BF16, name=f"diff_bf{cb}")
             for lo in range(0, N, PIECE):
                 nc.vector.tensor_tensor(
                     diff[:, lo : lo + PIECE],
                     tables[cb][:].indirect(offsets[:, lo // 16 : (lo + PIECE) // 16]), neg_e[:], ADD,
                 )
-            diff_bf = held.tile([P, N], BF16, name=f"diff_bf{cb}")
-            nc.vector.tensor_copy(diff_bf[:], diff[:])
+                if lo < by_scalar:
+                    nc.scalar.activation(diff_bf[:, lo : lo + PIECE], diff[:, lo : lo + PIECE], COPY)
+            nc.vector.tensor_copy(diff_bf[:, by_scalar:N], diff[:, by_scalar:N])
 
             weights = values[cb][:].rearrange("c (p mb) -> c mb p", mb=M_BLOCKS)
             for mb in range(M_BLOCKS):

@@ -46,7 +46,8 @@ def tile_pgd_kernel(tc, w_e, w_v, offs, out):
         def load_table(cb):
             lo = 0
             for width in load_widths(cb):
-                nc.sync.dma_start(tables[cb][:, lo : lo + width], w_e[cb * P : (cb + 1) * P, lo : lo + width])
+                queue = nc.scalar if cb < C_BLOCKS // 2 and lo > 0 else nc.sync
+                queue.dma_start(tables[cb][:, lo : lo + width], w_e[cb * P : (cb + 1) * P, lo : lo + width])
                 lo += width
 
         def load_values(cb):

@@ -65,12 +65,13 @@ def tile_pgd_kernel(tc, w_e, w_v, offs, out):
 
         for cb in range(C_BLOCKS):
             parts = work.tile([P, LINE], F32, name="parts")
-            earlier = work.tile([P, 1], F32, name="earlier")
+            earlier = parts
             newest = work.tile([P, 1], F32, name="newest")
             lo = 0
             last_k = len(load_widths(cb)) - 1
             for k, width in enumerate(load_widths(cb)):
-                if k == last_k:
+                if k == last_k and last_k > 1:
+                    earlier = work.tile([P, 1], F32, name="earlier")
                     nc.vector.tensor_reduce(out=earlier[:], in_=parts[:, 0:last_k], axis=X, op=ADD)
                 if lo < S // 2:
                     copied = work.tile([P, S // 2], F32, name="copied")

@@ -3,13 +3,14 @@ import concourse.mybir as mybir
 F32, BF16, U16 = mybir.dt.float32, mybir.dt.bfloat16, mybir.dt.uint16
 ADD, MULT = mybir.AluOpType.add, mybir.AluOpType.mult
 COPY = mybir.ActivationFunctionType.Copy
-X = mybir.AxisListType.X
 
 P = 128
 C, S, N, M = 512, 4096, 512, 1024
 EPS = 1e-8
 C_BLOCKS = C // P
 M_BLOCKS = M // P
+HALF = M_BLOCKS // 2
+MH = M // 2
 LINE = 8
 PIECE = 256
 
@@ -26,7 +27,7 @@ def store_ranges():
     ranges = [(0, N // 2)]
     while ranges[-1][1] < M_BLOCKS * N:
         hi = ranges[-1][1]
-        ranges.append((hi, 2 * hi))
+        ranges.append((hi, min(2 * hi, hi + 2 * N)))
     return ranges
 
 
@@ -41,7 +42,9 @@ def tile_pgd_kernel(tc, w_e, w_v, offs, out):
         nc.sync.dma_start(offsets[:], offs)
 
         tables = [held.tile([P, S], F32, name=f"table{cb}") for cb in range(C_BLOCKS)]
-        values = [held.tile([P, M], BF16, name=f"values{cb}") for cb in range(C_BLOCKS)]
+        outer_values = {cb: held.tile([P, M], BF16, name=f"values{cb}") for cb in (0, C_BLOCKS - 1)}
+        inner_values = [held.tile([P, C_BLOCKS - 2, MH], BF16, name=f"inner_values{h}") for h in range(2)]
+        value_rows = w_v.rearrange("(cb p) m -> p cb m", p=P)
 
         def load_table(cb):
             lo = 0
@@ -50,36 +53,53 @@ def tile_pgd_kernel(tc, w_e, w_v, offs, out):
                 queue.dma_start(tables[cb][:, lo : lo + width], w_e[cb * P : (cb + 1) * P, lo : lo + width])
                 lo += width
 
-        def load_values(cb):
-            nc.sync.dma_start(values[cb][:], w_v[cb * P : (cb + 1) * P, :])
+        def load_outer_values(cb):
+            nc.sync.dma_start(outer_values[cb][:], value_rows[:, cb, :])
+
+        def load_inner_values(h):
+            nc.sync.dma_start(inner_values[h][:], value_rows[:, 1 : C_BLOCKS - 1, h * MH : (h + 1) * MH])
 
         for cb in range(C_BLOCKS - 1):
             load_table(cb)
-        for cb in range(C_BLOCKS // 2):
-            load_values(cb)
+        load_outer_values(0)
+        load_inner_values(0)
         load_table(C_BLOCKS - 1)
-        for cb in range(C_BLOCKS // 2, C_BLOCKS):
-            load_values(cb)
+        load_inner_values(1)
+        load_outer_values(C_BLOCKS - 1)
 
         banks = [psum.tile([P, N], F32, name=f"bank{mb}") for mb in range(M_BLOCKS)]
 
-        for cb in range(C_BLOCKS):
+        def matmul(cb, mb, lo, hi):
+            h = mb // HALF
+            if cb in outer_values:
+                half_values = outer_values[cb][:, h * MH : (h + 1) * MH]
+            else:
+                half_values = inner_values[h][:, cb - 1, :]
+            weights = half_values.rearrange("c (p r) -> c r p", r=HALF)
+            nc.tensor.matmul(
+                banks[mb][:, lo:hi], weights[:, mb % HALF, :], diffs_bf[cb][:, lo:hi],
+                start=(cb == 0), stop=(cb == C_BLOCKS - 1 and hi == N),
+            )
+
+        def sum_on_scalar(cb):
             parts = work.tile([P, LINE], F32, name="parts")
-            earlier = parts
-            newest = work.tile([P, 1], F32, name="newest")
             lo = 0
-            last_k = len(load_widths(cb)) - 1
             for k, width in enumerate(load_widths(cb)):
-                if k == last_k and last_k > 1:
-                    earlier = work.tile([P, 1], F32, name="earlier")
-                    nc.vector.tensor_reduce(out=earlier[:], in_=parts[:, 0:last_k], axis=X, op=ADD)
                 if lo < S // 2:
                     copied = work.tile([P, S // 2], F32, name="copied")
                     nc.scalar.activation(
                         out=copied[:, 0:width], in_=tables[cb][:, lo : lo + width], func=COPY,
                         accum_out=parts[:, k : k + 1],
                     )
-                else:
+                lo += width
+            return parts
+
+        def sum_on_vector(cb, parts):
+            newest = work.tile([P, 1], F32, name="newest")
+            lo = 0
+            last_k = len(load_widths(cb)) - 1
+            for k, width in enumerate(load_widths(cb)):
+                if lo >= S // 2:
                     mid = lo + width // 2
                     folded = work.tile([P, S // 4], F32, name="folded")
                     nc.vector.scalar_tensor_tensor(
@@ -88,6 +108,22 @@ def tile_pgd_kernel(tc, w_e, w_v, offs, out):
                         accum_out=newest[:] if k == last_k else parts[:, k : k + 1],
                     )
                 lo += width
+            if last_k == 1:
+                return parts, newest
+            earlier = work.tile([P, 1], F32, name="earlier")
+            parts_copied = work.tile([P, LINE], F32, name="parts_copied")
+            nc.scalar.activation(
+                out=parts_copied[:, 0:last_k], in_=parts[:, 0:last_k], func=COPY, accum_out=earlier[:],
+            )
+            return earlier, newest
+
+        diffs_bf = []
+        next_parts = sum_on_scalar(0)
+        for cb in range(C_BLOCKS):
+            parts = next_parts
+            if cb < C_BLOCKS - 1:
+                next_parts = sum_on_scalar(cb + 1)
+            earlier, newest = sum_on_vector(cb, parts)
             neg_e = work.tile([P, PIECE], F32, name="neg_e")
             nc.vector.tensor_scalar(
                 out=neg_e[:], in0=earlier[:, 0:1].to_broadcast([P, PIECE]), scalar1=newest[:, 0:1],
@@ -95,26 +131,29 @@ def tile_pgd_kernel(tc, w_e, w_v, offs, out):
             )
 
             diff = work.tile([P, N], F32, name="diff")
-            by_scalar = N - PIECE if cb == C_BLOCKS - 1 else 0
             diff_bf = held.tile([P, N], BF16, name=f"diff_bf{cb}")
             for lo in range(0, N, PIECE):
                 nc.vector.tensor_tensor(
                     diff[:, lo : lo + PIECE],
                     tables[cb][:].indirect(offsets[:, lo // 16 : (lo + PIECE) // 16]), neg_e[:], ADD,
                 )
-                if lo < by_scalar:
+                if cb == C_BLOCKS - 1 and lo + PIECE == N:
+                    nc.vector.tensor_copy(diff_bf[:, lo : lo + PIECE], diff[:, lo : lo + PIECE])
+                else:
                     nc.scalar.activation(diff_bf[:, lo : lo + PIECE], diff[:, lo : lo + PIECE], COPY)
-            nc.vector.tensor_copy(diff_bf[:, by_scalar:N], diff[:, by_scalar:N])
+            diffs_bf.append(diff_bf)
 
-            weights = values[cb][:].rearrange("c (p mb) -> c mb p", mb=M_BLOCKS)
-            for mb in range(M_BLOCKS):
-                nc.tensor.matmul(
-                    banks[mb][:], weights[:, mb, :], diff_bf[:],
-                    start=(cb == 0), stop=(cb == C_BLOCKS - 1),
-                )
+            width = PIECE if cb == C_BLOCKS - 1 else N
+            for lo in range(0, N, width):
+                for mb in range(M_BLOCKS if cb == 0 else HALF):
+                    matmul(cb, mb, lo, lo + width)
+
+        for mb in range(HALF, M_BLOCKS):
+            for cb in range(1, C_BLOCKS):
+                matmul(cb, mb, 0, N)
 
         staged = held.tile([P, M_BLOCKS * N], F32, name="staged")
-        out_by_partition = out.rearrange("(p mb) j -> p (mb j)", mb=M_BLOCKS)
+        out_by_partition = out.rearrange("(h p r) j -> h p (r j)", h=2, p=P)
         for lo, hi in store_ranges():
             for a in range(lo, hi, N):
                 b = min(a + N, hi)
@@ -123,4 +162,5 @@ def tile_pgd_kernel(tc, w_e, w_v, offs, out):
                     nc.vector.tensor_copy(staged[:, a:b], banks[mb][:, a - mb * N : b - mb * N])
                 else:
                     nc.scalar.activation(staged[:, a:b], banks[mb][:, a - mb * N : b - mb * N], COPY)
-            nc.sync.dma_start(out_by_partition[:, lo:hi], staged[:, lo:hi])
+            h = lo // (HALF * N)
+            nc.sync.dma_start(out_by_partition[h, :, lo - h * HALF * N : hi - h * HALF * N], staged[:, lo:hi])

@@ -25,9 +25,12 @@ def load_widths(cb):
 
 def store_ranges():
     ranges = [(0, N // 2)]
-    while ranges[-1][1] < M_BLOCKS * N:
+    while ranges[-1][1] < HALF * N:
         hi = ranges[-1][1]
-        ranges.append((hi, min(2 * hi, hi + 2 * N)))
+        ranges.append((hi, 2 * hi))
+    for n_banks in (2, 1, 1):
+        hi = ranges[-1][1]
+        ranges.append((hi, hi + n_banks * N))
     return ranges
 
 
@@ -42,8 +45,8 @@ def tile_pgd_kernel(tc, w_e, w_v, offs, out):
         nc.sync.dma_start(offsets[:], offs)
 
         tables = [held.tile([P, S], F32, name=f"table{cb}") for cb in range(C_BLOCKS)]
-        outer_values = {cb: held.tile([P, M], BF16, name=f"values{cb}") for cb in (0, C_BLOCKS - 1)}
-        inner_values = [held.tile([P, C_BLOCKS - 2, MH], BF16, name=f"inner_values{h}") for h in range(2)]
+        first_values = [held.tile([P, C_BLOCKS - 1, MH], BF16, name=f"first_values{h}") for h in range(2)]
+        last_values = held.tile([P, M], BF16, name="last_values")
         value_rows = w_v.rearrange("(cb p) m -> p cb m", p=P)
 
         def load_table(cb):
@@ -53,28 +56,22 @@ def tile_pgd_kernel(tc, w_e, w_v, offs, out):
                 queue.dma_start(tables[cb][:, lo : lo + width], w_e[cb * P : (cb + 1) * P, lo : lo + width])
                 lo += width
 
-        def load_outer_values(cb):
-            nc.sync.dma_start(outer_values[cb][:], value_rows[:, cb, :])
-
-        def load_inner_values(h):
-            nc.sync.dma_start(inner_values[h][:], value_rows[:, 1 : C_BLOCKS - 1, h * MH : (h + 1) * MH])
-
         for cb in range(C_BLOCKS - 1):
             load_table(cb)
-        load_outer_values(0)
-        load_inner_values(0)
+        nc.sync.dma_start(first_values[0][:], value_rows[:, 0 : C_BLOCKS - 1, 0:MH])
         load_table(C_BLOCKS - 1)
-        load_inner_values(1)
-        load_outer_values(C_BLOCKS - 1)
+        for cb in range(C_BLOCKS - 1):
+            nc.sync.dma_start(first_values[1][:, cb, :], value_rows[:, cb, MH:M])
+        nc.sync.dma_start(last_values[:], value_rows[:, C_BLOCKS - 1, :])
 
         banks = [psum.tile([P, N], F32, name=f"bank{mb}") for mb in range(M_BLOCKS)]
 
         def matmul(cb, mb, lo, hi):
             h = mb // HALF
-            if cb in outer_values:
-                half_values = outer_values[cb][:, h * MH : (h + 1) * MH]
+            if cb < C_BLOCKS - 1:
+                half_values = first_values[h][:, cb, :]
             else:
-                half_values = inner_values[h][:, cb - 1, :]
+                half_values = last_values[:, h * MH : (h + 1) * MH]
             weights = half_values.rearrange("c (p r) -> c r p", r=HALF)
             nc.tensor.matmul(
                 banks[mb][:, lo:hi], weights[:, mb % HALF, :], diffs_bf[cb][:, lo:hi],
@@ -145,11 +142,11 @@ def tile_pgd_kernel(tc, w_e, w_v, offs, out):
 
             width = PIECE if cb == C_BLOCKS - 1 else N
             for lo in range(0, N, width):
-                for mb in range(M_BLOCKS if cb == 0 else HALF):
+                for mb in range(HALF):
                     matmul(cb, mb, lo, lo + width)
 
         for mb in range(HALF, M_BLOCKS):
-            for cb in range(1, C_BLOCKS):
+            for cb in range(C_BLOCKS):
                 matmul(cb, mb, 0, N)
 
         staged = held.tile([P, M_BLOCKS * N], F32, name="staged")

@@ -141,8 +141,8 @@ def tile_pgd_kernel(tc, w_e, w_v, offs, out):
             diffs_bf.append(diff_bf)
 
             width = PIECE if cb == C_BLOCKS - 1 else N
-            for lo in range(0, N, width):
-                for mb in range(HALF):
+            for mb in range(HALF):
+                for lo in range(0, N, width):
                     matmul(cb, mb, lo, lo + width)
 
         for mb in range(HALF, M_BLOCKS):

@@ -12,7 +12,8 @@ M_BLOCKS = M // P
 HALF = M_BLOCKS // 2
 MH = M // 2
 LINE = 8
-PIECE = 256
+PIECES = [(0, 5 * N // 8), (5 * N // 8, N)]
+WIDEST = max(hi - lo for lo, hi in PIECES)
 
 FLOPS = 2 * C * M * N
 
@@ -20,7 +21,7 @@ FLOPS = 2 * C * M * N
 def load_widths(cb):
     if cb < C_BLOCKS - 1:
         return [S // 2, S // 2]
-    return [S // 4, S // 4, S // 4, S // 8, S // 8]
+    return [S // 4, S // 4, S // 4, 5 * S // 32, 3 * S // 32]
 
 
 def store_ranges():
@@ -121,29 +122,27 @@ def tile_pgd_kernel(tc, w_e, w_v, offs, out):
             if cb < C_BLOCKS - 1:
                 next_parts = sum_on_scalar(cb + 1)
             earlier, newest = sum_on_vector(cb, parts)
-            neg_e = work.tile([P, PIECE], F32, name="neg_e")
+            neg_e = work.tile([P, WIDEST], F32, name="neg_e")
             nc.vector.tensor_scalar(
-                out=neg_e[:], in0=earlier[:, 0:1].to_broadcast([P, PIECE]), scalar1=newest[:, 0:1],
+                out=neg_e[:], in0=earlier[:, 0:1].to_broadcast([P, WIDEST]), scalar1=newest[:, 0:1],
                 scalar2=-1.0 / (S + EPS), op0=ADD, op1=MULT,
             )
 
             diff = work.tile([P, N], F32, name="diff")
             diff_bf = held.tile([P, N], BF16, name=f"diff_bf{cb}")
-            for lo in range(0, N, PIECE):
+            for lo, hi in PIECES:
                 nc.vector.tensor_tensor(
-                    diff[:, lo : lo + PIECE],
-                    tables[cb][:].indirect(offsets[:, lo // 16 : (lo + PIECE) // 16]), neg_e[:], ADD,
+                    diff[:, lo:hi], tables[cb][:].indirect(offsets[:, lo // 16 : hi // 16]), neg_e[:, 0 : hi - lo], ADD,
                 )
-                if cb == C_BLOCKS - 1 and lo + PIECE == N:
-                    nc.vector.tensor_copy(diff_bf[:, lo : lo + PIECE], diff[:, lo : lo + PIECE])
+                if cb == C_BLOCKS - 1 and hi == N:
+                    nc.vector.tensor_copy(diff_bf[:, lo:hi], diff[:, lo:hi])
                 else:
-                    nc.scalar.activation(diff_bf[:, lo : lo + PIECE], diff[:, lo : lo + PIECE], COPY)
+                    nc.scalar.activation(diff_bf[:, lo:hi], diff[:, lo:hi], COPY)
             diffs_bf.append(diff_bf)
 
-            width = PIECE if cb == C_BLOCKS - 1 else N
             for mb in range(HALF):
-                for lo in range(0, N, width):
-                    matmul(cb, mb, lo, lo + width)
+                for lo, hi in PIECES if cb == C_BLOCKS - 1 else [(0, N)]:
+                    matmul(cb, mb, lo, hi)
 
         for mb in range(HALF, M_BLOCKS):
             for cb in range(C_BLOCKS):

@@ -21,7 +21,22 @@ FLOPS = 2 * C * M * N
 def load_widths(cb):
     if cb < C_BLOCKS - 1:
         return [S // 2, S // 2]
-    return [S // 4, S // 4, S // 4, 5 * S // 32, 3 * S // 32]
+    return [S // 2, S // 4, 5 * S // 32, 3 * S // 32]
+
+
+def scalar_columns(cb):
+    return S // 2 if cb < C_BLOCKS - 1 else 3 * S // 8
+
+
+def vector_ranges(cb):
+    ranges = []
+    lo, hi = scalar_columns(cb), 0
+    for width in load_widths(cb):
+        hi += width
+        if lo < hi:
+            ranges.append((lo, hi))
+            lo = hi
+    return ranges
 
 
 def store_ranges():
@@ -43,7 +58,6 @@ def tile_pgd_kernel(tc, w_e, w_v, offs, out):
         tc.psum_pool(name="psum", bufs=1) as psum,
     ):
         offsets = held.tile([P, N // 16], U16, name="offsets")
-        nc.sync.dma_start(offsets[:], offs)
 
         tables = [held.tile([P, S], F32, name=f"table{cb}") for cb in range(C_BLOCKS)]
         first_values = [held.tile([P, C_BLOCKS - 1, MH], BF16, name=f"first_values{h}") for h in range(2)]
@@ -59,6 +73,8 @@ def tile_pgd_kernel(tc, w_e, w_v, offs, out):
 
         for cb in range(C_BLOCKS - 1):
             load_table(cb)
+            if cb == 0:
+                nc.sync.dma_start(offsets[:], offs)
         nc.sync.dma_start(first_values[0][:], value_rows[:, 0 : C_BLOCKS - 1, 0:MH])
         load_table(C_BLOCKS - 1)
         for cb in range(C_BLOCKS - 1):
@@ -81,37 +97,30 @@ def tile_pgd_kernel(tc, w_e, w_v, offs, out):
 
         def sum_on_scalar(cb):
             parts = work.tile([P, LINE], F32, name="parts")
-            lo = 0
-            for k, width in enumerate(load_widths(cb)):
-                if lo < S // 2:
-                    copied = work.tile([P, S // 2], F32, name="copied")
-                    nc.scalar.activation(
-                        out=copied[:, 0:width], in_=tables[cb][:, lo : lo + width], func=COPY,
-                        accum_out=parts[:, k : k + 1],
-                    )
-                lo += width
+            copied = work.tile([P, S // 2], F32, name="copied")
+            n_columns = scalar_columns(cb)
+            nc.scalar.activation(
+                out=copied[:, 0:n_columns], in_=tables[cb][:, 0:n_columns], func=COPY, accum_out=parts[:, 0:1],
+            )
             return parts
 
         def sum_on_vector(cb, parts):
             newest = work.tile([P, 1], F32, name="newest")
-            lo = 0
-            last_k = len(load_widths(cb)) - 1
-            for k, width in enumerate(load_widths(cb)):
-                if lo >= S // 2:
-                    mid = lo + width // 2
-                    folded = work.tile([P, S // 4], F32, name="folded")
-                    nc.vector.scalar_tensor_tensor(
-                        out=folded[:, 0 : width // 2], in0=tables[cb][:, lo:mid], scalar=1.0,
-                        in1=tables[cb][:, mid : lo + width], op0=MULT, op1=ADD,
-                        accum_out=newest[:] if k == last_k else parts[:, k : k + 1],
-                    )
-                lo += width
-            if last_k == 1:
+            ranges = vector_ranges(cb)
+            n_parts = len(ranges)
+            for k, (lo, hi) in enumerate(ranges, start=1):
+                mid = (lo + hi) // 2
+                folded = work.tile([P, S // 4], F32, name="folded")
+                nc.vector.scalar_tensor_tensor(
+                    out=folded[:, 0 : hi - mid], in0=tables[cb][:, lo:mid], scalar=1.0, in1=tables[cb][:, mid:hi],
+                    op0=MULT, op1=ADD, accum_out=newest[:] if k == n_parts else parts[:, k : k + 1],
+                )
+            if n_parts == 1:
                 return parts, newest
             earlier = work.tile([P, 1], F32, name="earlier")
             parts_copied = work.tile([P, LINE], F32, name="parts_copied")
             nc.scalar.activation(
-                out=parts_copied[:, 0:last_k], in_=parts[:, 0:last_k], func=COPY, accum_out=earlier[:],
+                out=parts_copied[:, 0:n_parts], in_=parts[:, 0:n_parts], func=COPY, accum_out=earlier[:],
             )
             return earlier, newest
 

@@ -75,8 +75,9 @@ def tile_pgd_kernel(tc, w_e, w_v, offs, out):
             load_table(cb)
             if cb == 0:
                 nc.sync.dma_start(offsets[:], offs)
-        nc.sync.dma_start(first_values[0][:], value_rows[:, 0 : C_BLOCKS - 1, 0:MH])
+        nc.sync.dma_start(first_values[0][:, 0:2, :], value_rows[:, 0:2, 0:MH])
         load_table(C_BLOCKS - 1)
+        nc.sync.dma_start(first_values[0][:, 2, :], value_rows[:, 2, 0:MH])
         for cb in range(C_BLOCKS - 1):
             nc.sync.dma_start(first_values[1][:, cb, :], value_rows[:, cb, MH:M])
         nc.sync.dma_start(last_values[:], value_rows[:, C_BLOCKS - 1, :])

import concourse.mybir as mybir

F32, BF16, U16 = mybir.dt.float32, mybir.dt.bfloat16, mybir.dt.uint16
ADD, MULT = mybir.AluOpType.add, mybir.AluOpType.mult
COPY = mybir.ActivationFunctionType.Copy

P = 128
C, S, N, M = 512, 4096, 512, 1024
EPS = 1e-8
C_BLOCKS = C // P
M_BLOCKS = M // P
HALF = M_BLOCKS // 2
MH = M // 2
LINE = 8
PIECES = [(0, 5 * N // 8), (5 * N // 8, N)]
WIDEST = max(hi - lo for lo, hi in PIECES)

FLOPS = 2 * C * M * N


def load_widths(cb):
    if cb < C_BLOCKS - 1:
        return [S // 2, S // 2]
    return [S // 2, S // 4, 5 * S // 32, 3 * S // 32]


def scalar_columns(cb):
    return S // 2 if cb < C_BLOCKS - 1 else 3 * S // 8


def vector_ranges(cb):
    ranges = []
    lo, hi = scalar_columns(cb), 0
    for width in load_widths(cb):
        hi += width
        if lo < hi:
            ranges.append((lo, hi))
            lo = hi
    return ranges


def store_ranges():
    ranges = [(0, N // 2)]
    while ranges[-1][1] < HALF * N:
        hi = ranges[-1][1]
        ranges.append((hi, 2 * hi))
    for n_banks in (2, 1, 1):
        hi = ranges[-1][1]
        ranges.append((hi, hi + n_banks * N))
    return ranges


def tile_pgd_kernel(tc, w_e, w_v, offs, out):
    nc = tc.nc
    with (
        tc.tile_pool(name="held", bufs=1) as held,
        tc.tile_pool(name="work", bufs=2) as work,
        tc.psum_pool(name="psum", bufs=1) as psum,
    ):
        offsets = held.tile([P, N // 16], U16, name="offsets")

        tables = [held.tile([P, S], F32, name=f"table{cb}") for cb in range(C_BLOCKS)]
        first_values = [held.tile([P, C_BLOCKS - 1, MH], BF16, name=f"first_values{h}") for h in range(2)]
        last_values = held.tile([P, M], BF16, name="last_values")
        value_rows = w_v.rearrange("(cb p) m -> p cb m", p=P)

        def load_table(cb):
            lo = 0
            for width in load_widths(cb):
                queue = nc.scalar if cb < C_BLOCKS // 2 and lo > 0 else nc.sync
                queue.dma_start(tables[cb][:, lo : lo + width], w_e[cb * P : (cb + 1) * P, lo : lo + width])
                lo += width

        for cb in range(C_BLOCKS - 1):
            load_table(cb)
            if cb == 0:
                nc.sync.dma_start(offsets[:], offs)
        nc.sync.dma_start(first_values[0][:, 0:2, :], value_rows[:, 0:2, 0:MH])
        load_table(C_BLOCKS - 1)
        nc.sync.dma_start(first_values[0][:, 2, :], value_rows[:, 2, 0:MH])
        for cb in range(C_BLOCKS - 1):
            nc.sync.dma_start(first_values[1][:, cb, :], value_rows[:, cb, MH:M])
        nc.sync.dma_start(last_values[:], value_rows[:, C_BLOCKS - 1, :])

        banks = [psum.tile([P, N], F32, name=f"bank{mb}") for mb in range(M_BLOCKS)]

        def matmul(cb, mb, lo, hi):
            h = mb // HALF
            if cb < C_BLOCKS - 1:
                half_values = first_values[h][:, cb, :]
            else:
                half_values = last_values[:, h * MH : (h + 1) * MH]
            weights = half_values.rearrange("c (p r) -> c r p", r=HALF)
            nc.tensor.matmul(
                banks[mb][:, lo:hi], weights[:, mb % HALF, :], diffs_bf[cb][:, lo:hi],
                start=(cb == 0), stop=(cb == C_BLOCKS - 1 and hi == N),
            )

        def sum_on_scalar(cb):
            parts = work.tile([P, LINE], F32, name="parts")
            copied = work.tile([P, S // 2], F32, name="copied")
            n_columns = scalar_columns(cb)
            nc.scalar.activation(
                out=copied[:, 0:n_columns], in_=tables[cb][:, 0:n_columns], func=COPY, accum_out=parts[:, 0:1],
            )
            return parts

        def sum_on_vector(cb, parts):
            newest = work.tile([P, 1], F32, name="newest")
            ranges = vector_ranges(cb)
            n_parts = len(ranges)
            for k, (lo, hi) in enumerate(ranges, start=1):
                mid = (lo + hi) // 2
                folded = work.tile([P, S // 4], F32, name="folded")
                nc.vector.scalar_tensor_tensor(
                    out=folded[:, 0 : hi - mid], in0=tables[cb][:, lo:mid], scalar=1.0, in1=tables[cb][:, mid:hi],
                    op0=MULT, op1=ADD, accum_out=newest[:] if k == n_parts else parts[:, k : k + 1],
                )
            if n_parts == 1:
                return parts, newest
            earlier = work.tile([P, 1], F32, name="earlier")
            parts_copied = work.tile([P, LINE], F32, name="parts_copied")
            nc.scalar.activation(
                out=parts_copied[:, 0:n_parts], in_=parts[:, 0:n_parts], func=COPY, accum_out=earlier[:],
            )
            return earlier, newest

        diffs_bf = []
        next_parts = sum_on_scalar(0)
        for cb in range(C_BLOCKS):
            parts = next_parts
            if cb < C_BLOCKS - 1:
                next_parts = sum_on_scalar(cb + 1)
            earlier, newest = sum_on_vector(cb, parts)
            neg_e = work.tile([P, WIDEST], F32, name="neg_e")
            nc.vector.tensor_scalar(
                out=neg_e[:], in0=earlier[:, 0:1].to_broadcast([P, WIDEST]), scalar1=newest[:, 0:1],
                scalar2=-1.0 / (S + EPS), op0=ADD, op1=MULT,
            )

            diff = work.tile([P, N], F32, name="diff")
            diff_bf = held.tile([P, N], BF16, name=f"diff_bf{cb}")
            for lo, hi in PIECES:
                nc.vector.tensor_tensor(
                    diff[:, lo:hi], tables[cb][:].indirect(offsets[:, lo // 16 : hi // 16]), neg_e[:, 0 : hi - lo], ADD,
                )
                if cb == C_BLOCKS - 1 and hi == N:
                    nc.vector.tensor_copy(diff_bf[:, lo:hi], diff[:, lo:hi])
                else:
                    nc.scalar.activation(diff_bf[:, lo:hi], diff[:, lo:hi], COPY)
            diffs_bf.append(diff_bf)

            for mb in range(HALF):
                for lo, hi in PIECES if cb == C_BLOCKS - 1 else [(0, N)]:
                    matmul(cb, mb, lo, hi)

        for mb in range(HALF, M_BLOCKS):
            for cb in range(C_BLOCKS):
                matmul(cb, mb, 0, N)

        staged = held.tile([P, M_BLOCKS * N], F32, name="staged")
        out_by_partition = out.rearrange("(h p r) j -> h p (r j)", h=2, p=P)
        for lo, hi in store_ranges():
            for a in range(lo, hi, N):
                b = min(a + N, hi)
                mb = a // N
                if mb % 2 == 0:
                    nc.vector.tensor_copy(staged[:, a:b], banks[mb][:, a - mb * N : b - mb * N])
                else:
                    nc.scalar.activation(staged[:, a:b], banks[mb][:, a - mb * N : b - mb * N], COPY)
            h = lo // (HALF * N)
            nc.sync.dma_start(out_by_partition[h, :, lo - h * HALF * N : hi - h * HALF * N], staged[:, lo:hi])
